import numpy as np
import ml_dtypes


BF16 = ml_dtypes.bfloat16


def bf(x):
    return np.asarray(x, np.float32).astype(BF16)


def f64(x):
    return np.asarray(x).astype(np.float64)


E2M1 = np.array([0.0, 0.5, 1.0, 1.5, 2.0, 3.0, 4.0, 6.0, -0.0, -0.5, -1.0, -1.5, -2.0, -3.0, -4.0, -6.0])


def pack_weight(w, fmt):
    k, n = w.shape
    w = f64(bf(w)).reshape(k // 32, 32, n)
    amax = np.abs(w).max(1)
    if fmt == "e4m3":
        byte = np.frexp(amax)[1] - 1 + 127 - 7
    else:
        mant, ex = np.frexp(amax / 6.0)
        byte = np.where(mant > 0.5, ex, ex - 1) + 127
    byte = np.clip(np.where(amax > 0, byte, 1), 1, 254)
    scaled = (w * np.exp2(127.0 - byte)[:, None, :]).reshape(k, n).astype(np.float32)
    by_word = np.ascontiguousarray(scaled.reshape(k // 512, 128, 4, n).transpose(0, 1, 3, 2))
    if fmt == "e4m3":
        words = by_word.astype(ml_dtypes.float8_e4m3fn).view(np.uint8)
    else:
        c = by_word.astype(ml_dtypes.float4_e2m1fn).view(np.uint8) & 0xF
        words = c[..., 0::2] | (c[..., 1::2] << 4)
    return np.ascontiguousarray(words), np.ascontiguousarray(byte.astype(np.uint8).reshape(k // 512, 16, n))


def unpack_weight(words, scales, fmt):
    g, p, n, _ = words.shape
    if fmt == "e4m3":
        vals = np.ascontiguousarray(words).view(ml_dtypes.float8_e4m3fn).astype(np.float64)
    else:
        nib = np.empty((g, p, n, 4), np.uint8)
        nib[..., 0::2] = words & 0xF
        nib[..., 1::2] = words >> 4
        vals = E2M1[nib]
    vals = vals * np.repeat(np.exp2(scales.astype(np.float64) - 127.0), 8, axis=1)[..., None]
    return vals.transpose(0, 1, 3, 2).reshape(g * 512, n)

def pack4(w):
    words, scales = pack_weight(w, "e2m1")
    return words.reshape(words.shape[0], 128, -1), scales


def unpack4(words, scales):
    return unpack_weight(words.reshape(words.shape[0], 128, -1, 2), scales, "e2m1")


def kspread(k):
    return np.exp2(np.repeat(np.random.randint(-6, 7, k // 32), 32).astype(np.float64))


S, HID, H, KV, D, WINDOW, QB = 512, 4096, 8, 4, 128, 512, 512
NQ, NK = H * D, KV * D
EPS = 1e-6
ROPE_THETA = 10000.0


def rms_norm(x, w):
    var = np.mean(x * x, axis=-1, keepdims=True)
    return x * (1.0 / np.sqrt(var + EPS)) * (1.0 + w)


def rotate_half(x):
    x1, x2 = np.split(x, 2, axis=-1)
    return np.concatenate([-x2, x1], axis=-1)


def apply_rope(x, cos, sin):
    return x * cos[:, None, :] + rotate_half(x) * sin[:, None, :]


def setup_inputs():
    s = kspread(HID)
    inv_freq = 1.0 / ROPE_THETA ** (np.arange(0, D, 2) / D)
    freqs = np.outer(np.arange(S), inv_freq)
    emb = np.concatenate([freqs, freqs], -1)
    hidden_states = np.random.standard_normal((S, HID)) * s
    hidden_states_words, hidden_states_scales = pack4(hidden_states.T)
    words, scales = pack4(np.random.standard_normal((HID, NQ + NK + NK)) / np.sqrt(HID) / s[:, None])
    return {"hidden_states_words": hidden_states_words, "hidden_states_scales": hidden_states_scales,
            "w_qkv_words": words, "w_qkv_scales": scales,
            "q_norm_w": bf(1.0 + 0.1 * np.random.standard_normal(D)),
            "k_norm_w": bf(1.0 + 0.1 * np.random.standard_normal(D)),
            "cos": bf(np.cos(emb)), "sin": bf(np.sin(emb))}


def reference(hidden_states_words, hidden_states_scales, w_qkv_words, w_qkv_scales, q_norm_w, k_norm_w, cos, sin):
    qkv = unpack4(hidden_states_words, hidden_states_scales).T @ unpack4(w_qkv_words, w_qkv_scales)
    q = qkv[:, :NQ].reshape(S, H, D)
    k = qkv[:, NQ:NQ + NK].reshape(S, KV, D)
    v = qkv[:, NQ + NK:].reshape(S, KV, D)
    q = rms_norm(q, f64(q_norm_w))
    k = rms_norm(k, f64(k_norm_w))
    q = apply_rope(q, f64(cos), f64(sin))
    k = apply_rope(k, f64(cos), f64(sin))
    return q, k, v

@@ -1,0 +1,263 @@
+from contextlib import ExitStack
+
+import concourse.mybir as mybir
+
+F32 = mybir.dt.float32
+BF16 = mybir.dt.bfloat16
+I32 = mybir.dt.int32
+U8 = mybir.dt.uint8
+FP4X4 = mybir.dt.float4_e2m1fn_x4
+ACT = mybir.ActivationFunctionType
+ALU = mybir.AluOpType
+
+P = 128
+S, HID, D = 512, 4096, 128
+NQ, NK = 1024, 512
+PASSES = HID // 512
+M_TILES = S // P
+BLOCK = 512
+HEADS = BLOCK // D
+EPS = 1e-6
+FIRST = 3
+WARM = 6
+
+FLOPS = 2 * S * HID * (NQ + 2 * NK)
+
+
+def tile_gemmaattention_pa_kernel(
+    tc, x_words, x_scales, w_words, w_scales, q_norm_w, k_norm_w, cos, sin, out_q, out_k, out_v
+):
+    nc = tc.nc
+    with ExitStack() as ctx:
+        keep = ctx.enter_context(tc.tile_pool(name="keep", bufs=1))
+        work = ctx.enter_context(tc.tile_pool(name="work", bufs=3))
+        psum = ctx.enter_context(tc.psum_pool(name="psum", bufs=8))
+        ctx.enter_context(tc.manual_schedule())
+
+        xc = keep.tile([P, PASSES, 2 * S], U8, align_bytes=64, name="xc")
+        xs = keep.tile([P, PASSES, S], U8, align_bytes=64, name="xs")
+        wc, ws = [], []
+        for n in range(4):
+            wc_n = keep.tile([P, PASSES, 2 * BLOCK], U8, align_bytes=64, name="wc%d" % n)
+            ws_n = keep.tile([P, PASSES, BLOCK], U8, align_bytes=64, name="ws%d" % n)
+            wc.append(wc_n)
+            ws.append(ws_n)
+        ones = keep.tile([P, P], BF16, align_bytes=64, name="ones")
+        zeros = keep.tile([P, 512], BF16, align_bytes=64, name="zeros")
+        wrow = keep.tile([P, 2 * D], BF16, align_bytes=64, name="wrow")
+        cos_sb = keep.tile([P, M_TILES, D], BF16, name="cos_sb")
+        sin_sb = keep.tile([P, M_TILES, D], BF16, name="sin_sb")
+        gain = keep.tile([P, 2, D], F32, name="gain")
+        gain_rot = keep.tile([P, 2, D], F32, name="gain_rot")
+        dummy = keep.tile([P, 1], F32, name="dummy")
+        c_tab, s_tab = [], []
+        for t in range(2):
+            c_t = keep.tile([P, M_TILES, D], F32, name="c_tab%d" % t)
+            s_t = keep.tile([P, M_TILES, D], F32, name="s_tab%d" % t)
+            c_tab.append(c_t)
+            s_tab.append(s_t)
+
+        def zero_plane(engine, plane, a, b):
+            engine.memset(plane[:, a:b, :].rearrange("p g n -> p (g n)").bitcast(I32), 0)
+
+        def load_x_codes(a, b):
+            nc.sync.dma_start(
+                out=xc[:, a:b, :].bitcast(I32), in_=x_words[a:b, :, :].rearrange("g p c -> p g c").bitcast(I32)
+            )
+
+        def load_w_codes(n, a, b):
+            nc.sync.dma_start(
+                out=wc[n][:, a:b, :].bitcast(I32),
+                in_=w_words[a:b, :, 2 * BLOCK * n : 2 * BLOCK * (n + 1)].rearrange("g p c -> p g c").bitcast(I32),
+            )
+
+        def load_x_scales(a, b):
+            for q in range(4):
+                nc.sync.dma_start(
+                    out=xs[32 * q : 32 * q + 4, a:b, :].bitcast(I32),
+                    in_=x_scales[a:b, 4 * q : 4 * q + 4, :].rearrange("g r n -> r g n").bitcast(I32),
+                )
+
+        def load_w_scales(n, a, b):
+            for q in range(4):
+                nc.sync.dma_start(
+                    out=ws[n][32 * q : 32 * q + 4, a:b, :].bitcast(I32),
+                    in_=w_scales[a:b, 4 * q : 4 * q + 4, BLOCK * n : BLOCK * (n + 1)]
+                    .rearrange("g r n -> r g n")
+                    .bitcast(I32),
+                )
+
+        zero_plane(nc.vector, xs, 0, FIRST)
+        nc.vector.memset(zeros[:], 0.0)
+        nc.vector.memset(ones[:], 1.0)
+        zero_plane(nc.vector, ws[0], 0, FIRST)
+        zero_plane(nc.vector, ws[1], 0, FIRST)
+        zero_plane(nc.vector, xs, FIRST, PASSES)
+        zero_plane(nc.vector, ws[0], FIRST, PASSES)
+        nc.gpsimd.memset(dummy[:], 1.0)
+        nc.gpsimd.memset(wrow[:], 0.0)
+        nc.gpsimd.dma_start(out=wrow[0:1, 0:D], in_=q_norm_w.unsqueeze(0))
+        nc.gpsimd.dma_start(out=wrow[0:1, D : 2 * D], in_=k_norm_w.unsqueeze(0))
+        zero_plane(nc.gpsimd, ws[1], FIRST, PASSES)
+        nc.gpsimd.dma_start(out=cos_sb[:], in_=cos.rearrange("(m p) d -> p m d", p=P))
+        nc.gpsimd.dma_start(out=sin_sb[:], in_=sin.rearrange("(m p) d -> p m d", p=P))
+        zero_plane(nc.gpsimd, ws[2], 0, PASSES)
+        zero_plane(nc.gpsimd, ws[3], 0, PASSES)
+        nc.scalar.activation(out=dummy[:], in_=dummy[:], func=ACT.Abs_reciprocal_sqrt)
+
+        load_x_codes(0, 1)
+        load_w_codes(0, 0, 1)
+        load_x_scales(0, FIRST)
+        load_w_scales(0, 0, FIRST)
+        load_x_codes(1, FIRST)
+        load_w_codes(0, 1, FIRST)
+        load_w_codes(1, 0, FIRST)
+        load_x_codes(FIRST, PASSES)
+        load_w_scales(1, 0, FIRST)
+        load_x_scales(FIRST, PASSES)
+        load_w_codes(0, FIRST, PASSES)
+        load_w_scales(0, FIRST, PASSES)
+        load_w_codes(1, FIRST, PASSES)
+        load_w_scales(1, FIRST, PASSES)
+        for n in (2, 3):
+            load_w_codes(n, 0, PASSES)
+            load_w_scales(n, 0, PASSES)
+
+        def multiply(acc, n, m, a, b, c0, c1):
+            for g in range(a, b):
+                nc.tensor.matmul_mx(
+                    out=acc[:, 0 : c1 - c0],
+                    lhsT=xc[:, g, 2 * P * m : 2 * P * (m + 1)].bitcast(FP4X4),
+                    lhsT_scale=xs[:, g, P * m : P * (m + 1)],
+                    rhs=wc[n][:, g, 2 * c0 : 2 * c1].bitcast(FP4X4),
+                    rhs_scale=ws[n][:, g, c0:c1],
+                    start=(g == 0),
+                    stop=(g == PASSES - 1),
+                )
+
+        def norm_rope(acc, n, m):
+            t = 0 if n < 2 else 1
+            sumsq = work.tile([P, HEADS], F32, name="sumsq")
+            rms = work.tile([P, HEADS], F32, name="rms")
+            junk = work.tile([P, D], BF16, name="junk")
+            for h in range(HEADS):
+                nc.scalar.activation(
+                    out=junk[:],
+                    in_=acc[:, D * h : D * (h + 1)],
+                    func=ACT.Square,
+                    accum_out=sumsq[:, h : h + 1],
+                )
+            nc.scalar.activation(out=rms[:], in_=sumsq[:], func=ACT.Abs_reciprocal_sqrt, scale=1.0 / D, bias=EPS)
+            straight = work.tile([P, BLOCK], F32, name="straight")
+            turned = work.tile([P, BLOCK], F32, name="turned")
+            nc.vector.tensor_tensor(
+                out=straight[:].rearrange("p (h d) -> p h d", h=HEADS),
+                in0=acc[:].rearrange("p (h d) -> p h d", h=HEADS),
+                in1=c_tab[t][:, m, :].unsqueeze(1).to_broadcast([P, HEADS, D]),
+                op=ALU.mult,
+            )
+            nc.vector.tensor_tensor(
+                out=turned[:].rearrange("p (h s d) -> p h s d", h=HEADS, s=2),
+                in0=acc[:].rearrange("p (h s d) -> p h s d", h=HEADS, s=2)[:, :, ::-1, :],
+                in1=s_tab[t][:, m, :]
+                .rearrange("p (s d) -> p s d", s=2)
+                .unsqueeze(1)
+                .to_broadcast([P, HEADS, 2, D // 2]),
+                op=ALU.mult,
+            )
+            total = work.tile([P, BLOCK], F32, name="total")
+            nc.vector.tensor_tensor(out=total[:], in0=straight[:], in1=turned[:], op=ALU.add)
+            return total, rms
+
+        def scale_store(total, rms, n, m):
+            result = work.tile([P, BLOCK], F32, name="result", bufs=4)
+            for h in range(HEADS):
+                nc.scalar.activation(
+                    out=result[:, D * h : D * (h + 1)],
+                    in_=total[:, D * h : D * (h + 1)],
+                    func=ACT.Copy,
+                    scale=rms[:, h : h + 1],
+                )
+            rows = slice(P * m, P * (m + 1))
+            if n < 2:
+                dst = out_q[rows, HEADS * n : HEADS * (n + 1), :]
+            else:
+                dst = out_k[rows, :, :]
+            nc.sync.dma_start(out=dst, in_=result[:].rearrange("p (h d) -> p h d", h=HEADS))
+
+        warm = psum.tile([P, BLOCK], F32, name="acc")
+        for i in range(WARM):
+            nc.tensor.matmul(out=warm[:], lhsT=ones[:], rhs=zeros[:], start=True, stop=True)
+
+        accs = {}
+        for n in (0, 1):
+            for m in range(M_TILES):
+                acc = psum.tile([P, BLOCK], F32, name="acc")
+                accs[(n, m)] = acc
+            if n == 0:
+                for g in range(FIRST):
+                    for m in range(M_TILES):
+                        multiply(accs[(n, m)], n, m, g, g + 1, 0, BLOCK)
+                spread = psum.tile([P, BLOCK], F32, name="acc")
+                nc.tensor.matmul(out=spread[:, 0 : 2 * D], lhsT=ones[:], rhs=wrow[:], start=True, stop=True)
+                nc.vector.tensor_scalar(
+                    out=gain[:].rearrange("p t d -> p (t d)"),
+                    in0=spread[:, 0 : 2 * D],
+                    scalar1=1.0,
+                    scalar2=None,
+                    op0=ALU.add,
+                )
+                half = D // 2
+                nc.vector.tensor_scalar(
+                    out=gain_rot[:, :, 0:half], in0=gain[:, :, half:D], scalar1=-1.0, scalar2=None, op0=ALU.mult
+                )
+                nc.vector.tensor_copy(out=gain_rot[:, :, half:D], in_=gain[:, :, 0:half])
+                for t in range(2):
+                    nc.vector.tensor_tensor(
+                        out=c_tab[t][:],
+                        in0=cos_sb[:],
+                        in1=gain[:, t, :].unsqueeze(1).to_broadcast([P, M_TILES, D]),
+                        op=ALU.mult,
+                    )
+                    nc.vector.tensor_tensor(
+                        out=s_tab[t][:],
+                        in0=sin_sb[:],
+                        in1=gain_rot[:, t, :].unsqueeze(1).to_broadcast([P, M_TILES, D]),
+                        op=ALU.mult,
+                    )
+            else:
+                for m in range(M_TILES):
+                    multiply(accs[(n, m)], n, m, 0, FIRST, 0, BLOCK)
+
+        pending = None
+        for n in range(3):
+            for m in range(M_TILES):
+                if n < 2:
+                    acc_nm = accs[(n, m)]
+                    multiply(acc_nm, n, m, FIRST, PASSES, 0, BLOCK)
+                else:
+                    acc_nm = psum.tile([P, BLOCK], F32, name="acc")
+                    multiply(acc_nm, n, m, 0, PASSES, 0, BLOCK)
+                total, rms = norm_rope(acc_nm, n, m)
+                if pending is not None:
+                    scale_store(*pending)
+                pending = (total, rms, n, m)
+
+        for m in range(M_TILES):
+            cuts = (0, 512) if m < M_TILES - 1 else (0, 256, 512)
+            for i in range(len(cuts) - 1):
+                c0, c1 = cuts[i], cuts[i + 1]
+                acc_v = psum.tile([P, BLOCK], F32, name="acc")
+                multiply(acc_v, 3, m, 0, PASSES, c0, c1)
+                if pending is not None:
+                    scale_store(*pending)
+                    pending = None
+                v_sb = work.tile([P, BLOCK], F32, name="v_sb", bufs=5)
+                if (m + i) % 2 == 0:
+                    nc.scalar.copy(out=v_sb[:, 0 : c1 - c0], in_=acc_v[:, 0 : c1 - c0])
+                else:
+                    nc.vector.tensor_copy(out=v_sb[:, 0 : c1 - c0], in_=acc_v[:, 0 : c1 - c0])
+                nc.sync.dma_start(
+                    out=out_v[P * m : P * (m + 1), c0 // D : c1 // D, :],
+                    in_=v_sb[:, 0 : c1 - c0].rearrange("p (h d) -> p h d", d=D),
+                )

@@ -16,10 +16,12 @@ NQ, NK = 1024, 512
 PASSES = HID // 512
 M_TILES = S // P
 BLOCK = 512
+HALF = 1024
 HEADS = BLOCK // D
 EPS = 1e-6
-FIRST = 3
-WARM = 6
+CUTS = (0, 2, 8)
+EARLY = 4
+WARM = 10
 
 FLOPS = 2 * S * HID * (NQ + 2 * NK)
 
@@ -35,13 +37,19 @@ def tile_gemmaattention_pa_kernel(
         ctx.enter_context(tc.manual_schedule())
 
         xc = keep.tile([P, PASSES, 2 * S], U8, align_bytes=64, name="xc")
-        xs = keep.tile([P, PASSES, S], U8, align_bytes=64, name="xs")
-        wc, ws = [], []
-        for n in range(4):
-            wc_n = keep.tile([P, PASSES, 2 * BLOCK], U8, align_bytes=64, name="wc%d" % n)
-            ws_n = keep.tile([P, PASSES, BLOCK], U8, align_bytes=64, name="ws%d" % n)
-            wc.append(wc_n)
-            ws.append(ws_n)
+        chunks = list(zip(CUTS[:-1], CUTS[1:]))
+        xs, ws0, wc = [], [], []
+        for a, b in chunks:
+            xs_c = keep.tile([P, b - a, S], U8, align_bytes=64, name="xs%d" % a)
+            ws_c = keep.tile([P, b - a, HALF], U8, align_bytes=64, name="ws0_%d" % a)
+            xs.append(xs_c)
+            ws0.append(ws_c)
+        ws1 = keep.tile([P, PASSES, HALF], U8, align_bytes=64, name="ws1")
+        for i in range(2):
+            wc_i = keep.tile([P, PASSES, 2 * HALF], U8, align_bytes=64, name="wc%d" % i)
+            wc.append(wc_i)
+        chunk_of = [c for c, (a, b) in enumerate(chunks) for g in range(a, b)]
+        index_in = [g - a for a, b in chunks for g in range(a, b)]
         ones = keep.tile([P, P], BF16, align_bytes=64, name="ones")
         zeros = keep.tile([P, 512], BF16, align_bytes=64, name="zeros")
         wrow = keep.tile([P, 2 * D], BF16, align_bytes=64, name="wrow")
@@ -57,88 +65,83 @@ def tile_gemmaattention_pa_kernel(
             c_tab.append(c_t)
             s_tab.append(s_t)
 
-        def zero_plane(engine, plane, a, b):
-            engine.memset(plane[:, a:b, :].rearrange("p g n -> p (g n)").bitcast(I32), 0)
+        def zero_plane(engine, plane):
+            engine.memset(plane[:].rearrange("p g n -> p (g n)").bitcast(I32), 0)
 
         def load_x_codes(a, b):
             nc.sync.dma_start(
                 out=xc[:, a:b, :].bitcast(I32), in_=x_words[a:b, :, :].rearrange("g p c -> p g c").bitcast(I32)
             )
 
-        def load_w_codes(n, a, b):
+        def load_w_codes(i, a, b):
             nc.sync.dma_start(
-                out=wc[n][:, a:b, :].bitcast(I32),
-                in_=w_words[a:b, :, 2 * BLOCK * n : 2 * BLOCK * (n + 1)].rearrange("g p c -> p g c").bitcast(I32),
+                out=wc[i][:, a:b, :].bitcast(I32),
+                in_=w_words[a:b, :, 2 * HALF * i : 2 * HALF * (i + 1)].rearrange("g p c -> p g c").bitcast(I32),
             )
 
-        def load_x_scales(a, b):
-            for q in range(4):
-                nc.sync.dma_start(
-                    out=xs[32 * q : 32 * q + 4, a:b, :].bitcast(I32),
-                    in_=x_scales[a:b, 4 * q : 4 * q + 4, :].rearrange("g r n -> r g n").bitcast(I32),
-                )
+        def scales_by_row(plane, src, a, b, c0, c1, r):
+            nc.sync.dma_start(
+                out=plane[r:P:32, :, :].bitcast(I32),
+                in_=src[a:b, r:16:4, c0:c1].rearrange("g q n -> q g n").bitcast(I32),
+            )
 
-        def load_w_scales(n, a, b):
-            for q in range(4):
-                nc.sync.dma_start(
-                    out=ws[n][32 * q : 32 * q + 4, a:b, :].bitcast(I32),
-                    in_=w_scales[a:b, 4 * q : 4 * q + 4, BLOCK * n : BLOCK * (n + 1)]
-                    .rearrange("g r n -> r g n")
-                    .bitcast(I32),
-                )
-
-        zero_plane(nc.vector, xs, 0, FIRST)
-        nc.vector.memset(zeros[:], 0.0)
-        nc.vector.memset(ones[:], 1.0)
-        zero_plane(nc.vector, ws[0], 0, FIRST)
-        zero_plane(nc.vector, ws[1], 0, FIRST)
-        zero_plane(nc.vector, xs, FIRST, PASSES)
-        zero_plane(nc.vector, ws[0], FIRST, PASSES)
+        zero_plane(nc.vector, xs[0])
+        zero_plane(nc.vector, ws0[0])
+        zero_plane(nc.vector, xs[1])
+        zero_plane(nc.vector, ws0[1])
+        nc.gpsimd.memset(zeros[:].bitcast(I32), 0)
+        nc.gpsimd.memset(ones[:], 1.0)
         nc.gpsimd.memset(dummy[:], 1.0)
         nc.gpsimd.memset(wrow[:], 0.0)
         nc.gpsimd.dma_start(out=wrow[0:1, 0:D], in_=q_norm_w.unsqueeze(0))
         nc.gpsimd.dma_start(out=wrow[0:1, D : 2 * D], in_=k_norm_w.unsqueeze(0))
-        zero_plane(nc.gpsimd, ws[1], FIRST, PASSES)
         nc.gpsimd.dma_start(out=cos_sb[:], in_=cos.rearrange("(m p) d -> p m d", p=P))
         nc.gpsimd.dma_start(out=sin_sb[:], in_=sin.rearrange("(m p) d -> p m d", p=P))
-        zero_plane(nc.gpsimd, ws[2], 0, PASSES)
-        zero_plane(nc.gpsimd, ws[3], 0, PASSES)
+        zero_plane(nc.gpsimd, ws1)
         nc.scalar.activation(out=dummy[:], in_=dummy[:], func=ACT.Abs_reciprocal_sqrt)
 
         load_x_codes(0, 1)
         load_w_codes(0, 0, 1)
-        load_x_scales(0, FIRST)
-        load_w_scales(0, 0, FIRST)
-        load_x_codes(1, FIRST)
-        load_w_codes(0, 1, FIRST)
-        load_w_codes(1, 0, FIRST)
-        load_x_codes(FIRST, PASSES)
-        load_w_scales(1, 0, FIRST)
-        load_x_scales(FIRST, PASSES)
-        load_w_codes(0, FIRST, PASSES)
-        load_w_scales(0, FIRST, PASSES)
-        load_w_codes(1, FIRST, PASSES)
-        load_w_scales(1, FIRST, PASSES)
-        for n in (2, 3):
-            load_w_codes(n, 0, PASSES)
-            load_w_scales(n, 0, PASSES)
+        for r in range(4):
+            scales_by_row(xs[0], x_scales, 0, CUTS[1], 0, S, r)
+        for r in range(4):
+            scales_by_row(ws0[0], w_scales, 0, CUTS[1], 0, HALF, r)
+        load_x_codes(1, CUTS[1])
+        load_w_codes(0, 1, CUTS[1])
+        for r in range(4):
+            scales_by_row(xs[1], x_scales, CUTS[1], PASSES, 0, S, r)
+            scales_by_row(ws0[1], w_scales, CUTS[1], PASSES, 0, HALF, r)
+        load_x_codes(CUTS[1], EARLY)
+        load_w_codes(0, CUTS[1], EARLY)
+        load_x_codes(EARLY, PASSES)
+        load_w_codes(0, EARLY, 6)
+        load_w_codes(0, 6, PASSES)
+        for r in range(4):
+            scales_by_row(ws1, w_scales, 0, PASSES, HALF, 2 * HALF, r)
+        load_w_codes(1, 0, 4)
+        load_w_codes(1, 4, PASSES)
 
         def multiply(acc, n, m, a, b, c0, c1):
+            i = n // 2
+            w0 = BLOCK * (n % 2) + c0
+            w1 = BLOCK * (n % 2) + c1
             for g in range(a, b):
+                c, j = chunk_of[g], index_in[g]
+                w_plane = ws0[c][:, j, w0:w1] if i == 0 else ws1[:, g, w0:w1]
                 nc.tensor.matmul_mx(
                     out=acc[:, 0 : c1 - c0],
                     lhsT=xc[:, g, 2 * P * m : 2 * P * (m + 1)].bitcast(FP4X4),
-                    lhsT_scale=xs[:, g, P * m : P * (m + 1)],
-                    rhs=wc[n][:, g, 2 * c0 : 2 * c1].bitcast(FP4X4),
-                    rhs_scale=ws[n][:, g, c0:c1],
+                    lhsT_scale=xs[c][:, j, P * m : P * (m + 1)],
+                    rhs=wc[i][:, g, 2 * w0 : 2 * w1].bitcast(FP4X4),
+                    rhs_scale=w_plane,
                     start=(g == 0),
                     stop=(g == PASSES - 1),
                 )
 
         def norm_rope(acc, n, m):
             t = 0 if n < 2 else 1
-            sumsq = work.tile([P, HEADS], F32, name="sumsq")
-            rms = work.tile([P, HEADS], F32, name="rms")
+            sumsq = work.tile([P, HEADS], F32, name="sumsq", bufs=4)
+            rms = work.tile([P, HEADS], F32, name="rms", bufs=5)
             junk = work.tile([P, D], BF16, name="junk")
             for h in range(HEADS):
                 nc.scalar.activation(
@@ -165,19 +168,27 @@ def tile_gemmaattention_pa_kernel(
                 .to_broadcast([P, HEADS, 2, D // 2]),
                 op=ALU.mult,
             )
-            total = work.tile([P, BLOCK], F32, name="total")
-            nc.vector.tensor_tensor(out=total[:], in0=straight[:], in1=turned[:], op=ALU.add)
+            total = work.tile([P, BLOCK], F32, name="total", bufs=5)
+            nc.gpsimd.tensor_tensor(out=total[:], in0=straight[:], in1=turned[:], op=ALU.add)
             return total, rms
 
         def scale_store(total, rms, n, m):
-            result = work.tile([P, BLOCK], F32, name="result", bufs=4)
-            for h in range(HEADS):
+            result = work.tile([P, BLOCK], F32, name="result", bufs=5)
+            for h in range(HEADS - 1):
                 nc.scalar.activation(
                     out=result[:, D * h : D * (h + 1)],
                     in_=total[:, D * h : D * (h + 1)],
                     func=ACT.Copy,
                     scale=rms[:, h : h + 1],
                 )
+            nc.gpsimd.tensor_scalar(
+                out=result[:, D * (HEADS - 1) : BLOCK],
+                in0=total[:, D * (HEADS - 1) : BLOCK],
+                scalar1=rms[:, HEADS - 1 : HEADS],
+                scalar2=0.0,
+                op0=ALU.mult,
+                op1=ALU.add,
+            )
             rows = slice(P * m, P * (m + 1))
             if n < 2:
                 dst = out_q[rows, HEADS * n : HEADS * (n + 1), :]
@@ -189,75 +200,67 @@ def tile_gemmaattention_pa_kernel(
         for i in range(WARM):
             nc.tensor.matmul(out=warm[:], lhsT=ones[:], rhs=zeros[:], start=True, stop=True)
 
+        early = [(n, m) for n in range(2) for m in range(M_TILES)][:-1]
         accs = {}
-        for n in (0, 1):
-            for m in range(M_TILES):
-                acc = psum.tile([P, BLOCK], F32, name="acc")
-                accs[(n, m)] = acc
-            if n == 0:
-                for g in range(FIRST):
-                    for m in range(M_TILES):
-                        multiply(accs[(n, m)], n, m, g, g + 1, 0, BLOCK)
-                spread = psum.tile([P, BLOCK], F32, name="acc")
-                nc.tensor.matmul(out=spread[:, 0 : 2 * D], lhsT=ones[:], rhs=wrow[:], start=True, stop=True)
-                nc.vector.tensor_scalar(
-                    out=gain[:].rearrange("p t d -> p (t d)"),
-                    in0=spread[:, 0 : 2 * D],
-                    scalar1=1.0,
-                    scalar2=None,
-                    op0=ALU.add,
-                )
-                half = D // 2
-                nc.vector.tensor_scalar(
-                    out=gain_rot[:, :, 0:half], in0=gain[:, :, half:D], scalar1=-1.0, scalar2=None, op0=ALU.mult
-                )
-                nc.vector.tensor_copy(out=gain_rot[:, :, half:D], in_=gain[:, :, 0:half])
-                for t in range(2):
-                    nc.vector.tensor_tensor(
-                        out=c_tab[t][:],
-                        in0=cos_sb[:],
-                        in1=gain[:, t, :].unsqueeze(1).to_broadcast([P, M_TILES, D]),
-                        op=ALU.mult,
-                    )
-                    nc.vector.tensor_tensor(
-                        out=s_tab[t][:],
-                        in0=sin_sb[:],
-                        in1=gain_rot[:, t, :].unsqueeze(1).to_broadcast([P, M_TILES, D]),
-                        op=ALU.mult,
-                    )
-            else:
-                for m in range(M_TILES):
-                    multiply(accs[(n, m)], n, m, 0, FIRST, 0, BLOCK)
+        for n, m in early:
+            acc = psum.tile([P, BLOCK], F32, name="acc")
+            accs[(n, m)] = acc
+        for g in range(EARLY):
+            for n, m in early:
+                multiply(accs[(n, m)], n, m, g, g + 1, 0, BLOCK)
 
-        pending = None
-        for n in range(3):
-            for m in range(M_TILES):
-                if n < 2:
-                    acc_nm = accs[(n, m)]
-                    multiply(acc_nm, n, m, FIRST, PASSES, 0, BLOCK)
-                else:
-                    acc_nm = psum.tile([P, BLOCK], F32, name="acc")
-                    multiply(acc_nm, n, m, 0, PASSES, 0, BLOCK)
-                total, rms = norm_rope(acc_nm, n, m)
-                if pending is not None:
-                    scale_store(*pending)
-                pending = (total, rms, n, m)
+        spread = psum.tile([P, BLOCK], F32, name="acc")
+        nc.tensor.matmul(out=spread[:, 0 : 2 * D], lhsT=ones[:], rhs=wrow[:], start=True, stop=True)
+        nc.vector.tensor_scalar(
+            out=gain[:].rearrange("p t d -> p (t d)"),
+            in0=spread[:, 0 : 2 * D],
+            scalar1=1.0,
+            scalar2=None,
+            op0=ALU.add,
+        )
+        half = D // 2
+        nc.vector.tensor_scalar(
+            out=gain_rot[:, :, 0:half], in0=gain[:, :, half:D], scalar1=-1.0, scalar2=None, op0=ALU.mult
+        )
+        nc.vector.tensor_copy(out=gain_rot[:, :, half:D], in_=gain[:, :, 0:half])
+        for t in range(2):
+            nc.vector.tensor_tensor(
+                out=c_tab[t][:],
+                in0=cos_sb[:],
+                in1=gain[:, t, :].unsqueeze(1).to_broadcast([P, M_TILES, D]),
+                op=ALU.mult,
+            )
+            nc.vector.tensor_tensor(
+                out=s_tab[t][:],
+                in0=sin_sb[:],
+                in1=gain_rot[:, t, :].unsqueeze(1).to_broadcast([P, M_TILES, D]),
+                op=ALU.mult,
+            )
 
-        for m in range(M_TILES):
-            cuts = (0, 512) if m < M_TILES - 1 else (0, 256, 512)
-            for i in range(len(cuts) - 1):
-                c0, c1 = cuts[i], cuts[i + 1]
-                acc_v = psum.tile([P, BLOCK], F32, name="acc")
-                multiply(acc_v, 3, m, 0, PASSES, c0, c1)
-                if pending is not None:
-                    scale_store(*pending)
-                    pending = None
-                v_sb = work.tile([P, BLOCK], F32, name="v_sb", bufs=5)
-                if (m + i) % 2 == 0:
-                    nc.scalar.copy(out=v_sb[:, 0 : c1 - c0], in_=acc_v[:, 0 : c1 - c0])
-                else:
+        order = early + [(1, 3), (2, 0), (2, 1), (3, 0), (2, 2), (2, 3), (3, 1), (3, 2), (3, 3)]
+        pending = []
+        for n, m in order:
+            if n == 3:
+                cuts = (0, 512) if m < M_TILES - 1 else (0, 256, 512)
+                for c0, c1 in zip(cuts[:-1], cuts[1:]):
+                    acc_v = psum.tile([P, BLOCK], F32, name="acc")
+                    multiply(acc_v, 3, m, 0, PASSES, c0, c1)
+                    if pending:
+                        scale_store(*pending.pop(0))
+                    v_sb = work.tile([P, BLOCK], F32, name="v_sb", bufs=5)
                     nc.vector.tensor_copy(out=v_sb[:, 0 : c1 - c0], in_=acc_v[:, 0 : c1 - c0])
-                nc.sync.dma_start(
-                    out=out_v[P * m : P * (m + 1), c0 // D : c1 // D, :],
-                    in_=v_sb[:, 0 : c1 - c0].rearrange("p (h d) -> p h d", d=D),
-                )
+                    nc.sync.dma_start(
+                        out=out_v[P * m : P * (m + 1), c0 // D : c1 // D, :],
+                        in_=v_sb[:, 0 : c1 - c0].rearrange("p (h d) -> p h d", d=D),
+                    )
+                continue
+            if (n, m) in accs:
+                acc_nm = accs[(n, m)]
+                multiply(acc_nm, n, m, EARLY, PASSES, 0, BLOCK)
+            else:
+                acc_nm = psum.tile([P, BLOCK], F32, name="acc")
+                multiply(acc_nm, n, m, 0, PASSES, 0, BLOCK)
+            total, rms = norm_rope(acc_nm, n, m)
+            if len(pending) == 2:
+                scale_store(*pending.pop(0))
+            pending.append((total, rms, n, m))

@@ -52,7 +52,10 @@ def tile_gemmaattention_pa_kernel(
         index_in = [g - a for a, b in chunks for g in range(a, b)]
         ones = keep.tile([P, P], BF16, align_bytes=64, name="ones")
         zeros = keep.tile([P, 512], BF16, align_bytes=64, name="zeros")
-        wrow = keep.tile([P, 2 * D], BF16, align_bytes=64, name="wrow")
+        w_rows = []
+        for t in range(2):
+            w_row = keep.tile([P, D], BF16, align_bytes=64, name="w_row%d" % t)
+            w_rows.append(w_row)
         cos_sb = keep.tile([P, M_TILES, D], BF16, name="cos_sb")
         sin_sb = keep.tile([P, M_TILES, D], BF16, name="sin_sb")
         gain = keep.tile([P, 2, D], F32, name="gain")
@@ -85,19 +88,19 @@ def tile_gemmaattention_pa_kernel(
                 in_=src[a:b, r:16:4, c0:c1].rearrange("g q n -> q g n").bitcast(I32),
             )
 
-        zero_plane(nc.vector, xs[0])
-        zero_plane(nc.vector, ws0[0])
-        zero_plane(nc.vector, xs[1])
-        zero_plane(nc.vector, ws0[1])
-        nc.gpsimd.memset(zeros[:].bitcast(I32), 0)
-        nc.gpsimd.memset(ones[:], 1.0)
-        nc.gpsimd.memset(dummy[:], 1.0)
-        nc.gpsimd.memset(wrow[:], 0.0)
-        nc.gpsimd.dma_start(out=wrow[0:1, 0:D], in_=q_norm_w.unsqueeze(0))
-        nc.gpsimd.dma_start(out=wrow[0:1, D : 2 * D], in_=k_norm_w.unsqueeze(0))
+        for t in range(2):
+            nc.vector.memset(w_rows[t][:].bitcast(I32), 0)
+        nc.vector.memset(zeros[:].bitcast(I32), 0)
+        nc.vector.memset(ones[:], 1.0)
+        for c in range(2):
+            zero_plane(nc.vector, xs[c])
+            zero_plane(nc.vector, ws0[c])
+        nc.vector.memset(dummy[:], 1.0)
+        zero_plane(nc.vector, ws1)
+        nc.gpsimd.dma_start(out=w_rows[0][0:1, :], in_=q_norm_w.unsqueeze(0))
+        nc.gpsimd.dma_start(out=w_rows[1][0:1, :], in_=k_norm_w.unsqueeze(0))
         nc.gpsimd.dma_start(out=cos_sb[:], in_=cos.rearrange("(m p) d -> p m d", p=P))
         nc.gpsimd.dma_start(out=sin_sb[:], in_=sin.rearrange("(m p) d -> p m d", p=P))
-        zero_plane(nc.gpsimd, ws1)
         nc.scalar.activation(out=dummy[:], in_=dummy[:], func=ACT.Abs_reciprocal_sqrt)
 
         load_x_codes(0, 1)
@@ -181,13 +184,12 @@ def tile_gemmaattention_pa_kernel(
                     func=ACT.Copy,
                     scale=rms[:, h : h + 1],
                 )
-            nc.gpsimd.tensor_scalar(
+            nc.vector.tensor_scalar(
                 out=result[:, D * (HEADS - 1) : BLOCK],
                 in0=total[:, D * (HEADS - 1) : BLOCK],
                 scalar1=rms[:, HEADS - 1 : HEADS],
-                scalar2=0.0,
+                scalar2=None,
                 op0=ALU.mult,
-                op1=ALU.add,
             )
             rows = slice(P * m, P * (m + 1))
             if n < 2:
@@ -205,12 +207,15 @@ def tile_gemmaattention_pa_kernel(
         for n, m in early:
             acc = psum.tile([P, BLOCK], F32, name="acc")
             accs[(n, m)] = acc
-        for g in range(EARLY):
+        for g in range(2):
             for n, m in early:
                 multiply(accs[(n, m)], n, m, g, g + 1, 0, BLOCK)
 
         spread = psum.tile([P, BLOCK], F32, name="acc")
-        nc.tensor.matmul(out=spread[:, 0 : 2 * D], lhsT=ones[:], rhs=wrow[:], start=True, stop=True)
+        for t in range(2):
+            nc.tensor.matmul(
+                out=spread[:, D * t : D * (t + 1)], lhsT=ones[:], rhs=w_rows[t][:], start=True, stop=True
+            )
         nc.vector.tensor_scalar(
             out=gain[:].rearrange("p t d -> p (t d)"),
             in0=spread[:, 0 : 2 * D],
@@ -236,6 +241,10 @@ def tile_gemmaattention_pa_kernel(
                 in1=gain_rot[:, t, :].unsqueeze(1).to_broadcast([P, M_TILES, D]),
                 op=ALU.mult,
             )
+
+        for g in range(2, EARLY):
+            for n, m in early:
+                multiply(accs[(n, m)], n, m, g, g + 1, 0, BLOCK)
 
         order = early + [(1, 3), (2, 0), (2, 1), (3, 0), (2, 2), (2, 3), (3, 1), (3, 2), (3, 3)]
         pending = []

from contextlib import ExitStack

import concourse.mybir as mybir

F32 = mybir.dt.float32
BF16 = mybir.dt.bfloat16
I32 = mybir.dt.int32
U8 = mybir.dt.uint8
FP4X4 = mybir.dt.float4_e2m1fn_x4
ACT = mybir.ActivationFunctionType
ALU = mybir.AluOpType

P = 128
S, HID, D = 512, 4096, 128
NQ, NK = 1024, 512
PASSES = HID // 512
M_TILES = S // P
BLOCK = 512
HALF = 1024
HEADS = BLOCK // D
EPS = 1e-6
CUTS = (0, 2, 8)
EARLY = 4
WARM = 10

FLOPS = 2 * S * HID * (NQ + 2 * NK)


def tile_gemmaattention_pa_kernel(
    tc, x_words, x_scales, w_words, w_scales, q_norm_w, k_norm_w, cos, sin, out_q, out_k, out_v
):
    nc = tc.nc
    with ExitStack() as ctx:
        keep = ctx.enter_context(tc.tile_pool(name="keep", bufs=1))
        work = ctx.enter_context(tc.tile_pool(name="work", bufs=3))
        psum = ctx.enter_context(tc.psum_pool(name="psum", bufs=8))
        ctx.enter_context(tc.manual_schedule())

        xc = keep.tile([P, PASSES, 2 * S], U8, align_bytes=64, name="xc")
        chunks = list(zip(CUTS[:-1], CUTS[1:]))
        xs, ws0, wc = [], [], []
        for a, b in chunks:
            xs_c = keep.tile([P, b - a, S], U8, align_bytes=64, name="xs%d" % a)
            ws_c = keep.tile([P, b - a, HALF], U8, align_bytes=64, name="ws0_%d" % a)
            xs.append(xs_c)
            ws0.append(ws_c)
        ws1 = keep.tile([P, PASSES, HALF], U8, align_bytes=64, name="ws1")
        for i in range(2):
            wc_i = keep.tile([P, PASSES, 2 * HALF], U8, align_bytes=64, name="wc%d" % i)
            wc.append(wc_i)
        chunk_of = [c for c, (a, b) in enumerate(chunks) for g in range(a, b)]
        index_in = [g - a for a, b in chunks for g in range(a, b)]
        ones = keep.tile([P, P], BF16, align_bytes=64, name="ones")
        zeros = keep.tile([P, 512], BF16, align_bytes=64, name="zeros")
        w_rows = []
        for t in range(2):
            w_row = keep.tile([P, D], BF16, align_bytes=64, name="w_row%d" % t)
            w_rows.append(w_row)
        cos_sb = keep.tile([P, M_TILES, D], BF16, name="cos_sb")
        sin_sb = keep.tile([P, M_TILES, D], BF16, name="sin_sb")
        gain = keep.tile([P, 2, D], F32, name="gain")
        gain_rot = keep.tile([P, 2, D], F32, name="gain_rot")
        dummy = keep.tile([P, 1], F32, name="dummy")
        c_tab, s_tab = [], []
        for t in range(2):
            c_t = keep.tile([P, M_TILES, D], F32, name="c_tab%d" % t)
            s_t = keep.tile([P, M_TILES, D], F32, name="s_tab%d" % t)
            c_tab.append(c_t)
            s_tab.append(s_t)

        def zero_plane(engine, plane):
            engine.memset(plane[:].rearrange("p g n -> p (g n)").bitcast(I32), 0)

        def load_x_codes(a, b):
            nc.sync.dma_start(
                out=xc[:, a:b, :].bitcast(I32), in_=x_words[a:b, :, :].rearrange("g p c -> p g c").bitcast(I32)
            )

        def load_w_codes(i, a, b):
            nc.sync.dma_start(
                out=wc[i][:, a:b, :].bitcast(I32),
                in_=w_words[a:b, :, 2 * HALF * i : 2 * HALF * (i + 1)].rearrange("g p c -> p g c").bitcast(I32),
            )

        def scales_by_row(plane, src, a, b, c0, c1, r):
            nc.sync.dma_start(
                out=plane[r:P:32, :, :].bitcast(I32),
                in_=src[a:b, r:16:4, c0:c1].rearrange("g q n -> q g n").bitcast(I32),
            )

        for t in range(2):
            nc.vector.memset(w_rows[t][:].bitcast(I32), 0)
        nc.vector.memset(zeros[:].bitcast(I32), 0)
        nc.vector.memset(ones[:], 1.0)
        for c in range(2):
            zero_plane(nc.vector, xs[c])
            zero_plane(nc.vector, ws0[c])
        nc.vector.memset(dummy[:], 1.0)
        zero_plane(nc.vector, ws1)
        nc.gpsimd.dma_start(out=w_rows[0][0:1, :], in_=q_norm_w.unsqueeze(0))
        nc.gpsimd.dma_start(out=w_rows[1][0:1, :], in_=k_norm_w.unsqueeze(0))
        nc.gpsimd.dma_start(out=cos_sb[:], in_=cos.rearrange("(m p) d -> p m d", p=P))
        nc.gpsimd.dma_start(out=sin_sb[:], in_=sin.rearrange("(m p) d -> p m d", p=P))
        nc.scalar.activation(out=dummy[:], in_=dummy[:], func=ACT.Abs_reciprocal_sqrt)

        load_x_codes(0, 1)
        load_w_codes(0, 0, 1)
        for r in range(4):
            scales_by_row(xs[0], x_scales, 0, CUTS[1], 0, S, r)
        for r in range(4):
            scales_by_row(ws0[0], w_scales, 0, CUTS[1], 0, HALF, r)
        load_x_codes(1, CUTS[1])
        load_w_codes(0, 1, CUTS[1])
        for r in range(4):
            scales_by_row(xs[1], x_scales, CUTS[1], PASSES, 0, S, r)
            scales_by_row(ws0[1], w_scales, CUTS[1], PASSES, 0, HALF, r)
        load_x_codes(CUTS[1], EARLY)
        load_w_codes(0, CUTS[1], EARLY)
        load_x_codes(EARLY, PASSES)
        load_w_codes(0, EARLY, 6)
        load_w_codes(0, 6, PASSES)
        for r in range(4):
            scales_by_row(ws1, w_scales, 0, PASSES, HALF, 2 * HALF, r)
        load_w_codes(1, 0, 4)
        load_w_codes(1, 4, PASSES)

        def multiply(acc, n, m, a, b, c0, c1):
            i = n // 2
            w0 = BLOCK * (n % 2) + c0
            w1 = BLOCK * (n % 2) + c1
            for g in range(a, b):
                c, j = chunk_of[g], index_in[g]
                w_plane = ws0[c][:, j, w0:w1] if i == 0 else ws1[:, g, w0:w1]
                nc.tensor.matmul_mx(
                    out=acc[:, 0 : c1 - c0],
                    lhsT=xc[:, g, 2 * P * m : 2 * P * (m + 1)].bitcast(FP4X4),
                    lhsT_scale=xs[c][:, j, P * m : P * (m + 1)],
                    rhs=wc[i][:, g, 2 * w0 : 2 * w1].bitcast(FP4X4),
                    rhs_scale=w_plane,
                    start=(g == 0),
                    stop=(g == PASSES - 1),
                )

        def norm_rope(acc, n, m):
            t = 0 if n < 2 else 1
            sumsq = work.tile([P, HEADS], F32, name="sumsq", bufs=4)
            rms = work.tile([P, HEADS], F32, name="rms", bufs=5)
            junk = work.tile([P, D], BF16, name="junk")
            for h in range(HEADS):
                nc.scalar.activation(
                    out=junk[:],
                    in_=acc[:, D * h : D * (h + 1)],
                    func=ACT.Square,
                    accum_out=sumsq[:, h : h + 1],
                )
            nc.scalar.activation(out=rms[:], in_=sumsq[:], func=ACT.Abs_reciprocal_sqrt, scale=1.0 / D, bias=EPS)
            straight = work.tile([P, BLOCK], F32, name="straight")
            turned = work.tile([P, BLOCK], F32, name="turned")
            nc.vector.tensor_tensor(
                out=straight[:].rearrange("p (h d) -> p h d", h=HEADS),
                in0=acc[:].rearrange("p (h d) -> p h d", h=HEADS),
                in1=c_tab[t][:, m, :].unsqueeze(1).to_broadcast([P, HEADS, D]),
                op=ALU.mult,
            )
            nc.vector.tensor_tensor(
                out=turned[:].rearrange("p (h s d) -> p h s d", h=HEADS, s=2),
                in0=acc[:].rearrange("p (h s d) -> p h s d", h=HEADS, s=2)[:, :, ::-1, :],
                in1=s_tab[t][:, m, :]
                .rearrange("p (s d) -> p s d", s=2)
                .unsqueeze(1)
                .to_broadcast([P, HEADS, 2, D // 2]),
                op=ALU.mult,
            )
            total = work.tile([P, BLOCK], F32, name="total", bufs=5)
            nc.gpsimd.tensor_tensor(out=total[:], in0=straight[:], in1=turned[:], op=ALU.add)
            return total, rms

        def scale_store(total, rms, n, m):
            result = work.tile([P, BLOCK], F32, name="result", bufs=5)
            for h in range(HEADS - 1):
                nc.scalar.activation(
                    out=result[:, D * h : D * (h + 1)],
                    in_=total[:, D * h : D * (h + 1)],
                    func=ACT.Copy,
                    scale=rms[:, h : h + 1],
                )
            nc.vector.tensor_scalar(
                out=result[:, D * (HEADS - 1) : BLOCK],
                in0=total[:, D * (HEADS - 1) : BLOCK],
                scalar1=rms[:, HEADS - 1 : HEADS],
                scalar2=None,
                op0=ALU.mult,
            )
            rows = slice(P * m, P * (m + 1))
            if n < 2:
                dst = out_q[rows, HEADS * n : HEADS * (n + 1), :]
            else:
                dst = out_k[rows, :, :]
            nc.sync.dma_start(out=dst, in_=result[:].rearrange("p (h d) -> p h d", h=HEADS))

        warm = psum.tile([P, BLOCK], F32, name="acc")
        for i in range(WARM):
            nc.tensor.matmul(out=warm[:], lhsT=ones[:], rhs=zeros[:], start=True, stop=True)

        early = [(n, m) for n in range(2) for m in range(M_TILES)][:-1]
        accs = {}
        for n, m in early:
            acc = psum.tile([P, BLOCK], F32, name="acc")
            accs[(n, m)] = acc
        for g in range(2):
            for n, m in early:
                multiply(accs[(n, m)], n, m, g, g + 1, 0, BLOCK)

        spread = psum.tile([P, BLOCK], F32, name="acc")
        for t in range(2):
            nc.tensor.matmul(
                out=spread[:, D * t : D * (t + 1)], lhsT=ones[:], rhs=w_rows[t][:], start=True, stop=True
            )
        nc.vector.tensor_scalar(
            out=gain[:].rearrange("p t d -> p (t d)"),
            in0=spread[:, 0 : 2 * D],
            scalar1=1.0,
            scalar2=None,
            op0=ALU.add,
        )
        half = D // 2
        nc.vector.tensor_scalar(
            out=gain_rot[:, :, 0:half], in0=gain[:, :, half:D], scalar1=-1.0, scalar2=None, op0=ALU.mult
        )
        nc.vector.tensor_copy(out=gain_rot[:, :, half:D], in_=gain[:, :, 0:half])
        for t in range(2):
            nc.vector.tensor_tensor(
                out=c_tab[t][:],
                in0=cos_sb[:],
                in1=gain[:, t, :].unsqueeze(1).to_broadcast([P, M_TILES, D]),
                op=ALU.mult,
            )
            nc.vector.tensor_tensor(
                out=s_tab[t][:],
                in0=sin_sb[:],
                in1=gain_rot[:, t, :].unsqueeze(1).to_broadcast([P, M_TILES, D]),
                op=ALU.mult,
            )

        for g in range(2, EARLY):
            for n, m in early:
                multiply(accs[(n, m)], n, m, g, g + 1, 0, BLOCK)

        order = early + [(1, 3), (2, 0), (2, 1), (3, 0), (2, 2), (2, 3), (3, 1), (3, 2), (3, 3)]
        pending = []
        for n, m in order:
            if n == 3:
                cuts = (0, 512) if m < M_TILES - 1 else (0, 256, 512)
                for c0, c1 in zip(cuts[:-1], cuts[1:]):
                    acc_v = psum.tile([P, BLOCK], F32, name="acc")
                    multiply(acc_v, 3, m, 0, PASSES, c0, c1)
                    if pending:
                        scale_store(*pending.pop(0))
                    v_sb = work.tile([P, BLOCK], F32, name="v_sb", bufs=5)
                    nc.vector.tensor_copy(out=v_sb[:, 0 : c1 - c0], in_=acc_v[:, 0 : c1 - c0])
                    nc.sync.dma_start(
                        out=out_v[P * m : P * (m + 1), c0 // D : c1 // D, :],
                        in_=v_sb[:, 0 : c1 - c0].rearrange("p (h d) -> p h d", d=D),
                    )
                continue
            if (n, m) in accs:
                acc_nm = accs[(n, m)]
                multiply(acc_nm, n, m, EARLY, PASSES, 0, BLOCK)
            else:
                acc_nm = psum.tile([P, BLOCK], F32, name="acc")
                multiply(acc_nm, n, m, 0, PASSES, 0, BLOCK)
            total, rms = norm_rope(acc_nm, n, m)
            if len(pending) == 2:
                scale_store(*pending.pop(0))
            pending.append((total, rms, n, m))
